import numpy as np
import ml_dtypes


def mxq(x, axis, fmt="e4m3"):
    dtype, down = {"e4m3": (ml_dtypes.float8_e4m3fn, 7), "e5m2": (ml_dtypes.float8_e5m2, 14)}[fmt]
    v = np.moveaxis(np.asarray(x, np.float32).astype(ml_dtypes.bfloat16).astype(np.float64), axis, -1)
    blocks = v.reshape(v.shape[:-1] + (-1, 32))
    amax = np.abs(blocks).max(-1, keepdims=True)
    byte = np.maximum(np.where(amax > 0, np.frexp(amax)[1] - 1 + 127, 0) - down, 1)
    scale = np.exp2(byte - 127.0)
    codes = (blocks / scale).astype(np.float32).astype(dtype).astype(np.float64)
    return np.moveaxis((codes * scale).reshape(v.shape), -1, axis)


WIDE = False


def mx_kscale(k):
    if not WIDE:
        return np.ones(k)
    levels = np.array([10, -10, 5, -5, 0])
    a = np.random.permutation(np.resize(levels, k // 512 * 4)).reshape(k // 512, 4)
    idx = np.arange(k)
    return np.exp2(a[idx // 512, idx % 128 // 32])


BF16 = ml_dtypes.bfloat16


def bf(x):
    return np.asarray(x, np.float32).astype(BF16)


def f64(x):
    return np.asarray(x).astype(np.float64)


E2M1 = np.array([0.0, 0.5, 1.0, 1.5, 2.0, 3.0, 4.0, 6.0, -0.0, -0.5, -1.0, -1.5, -2.0, -3.0, -4.0, -6.0])


def pack_weight(w, fmt):
    k, n = w.shape
    w = f64(bf(w)).reshape(k // 32, 32, n)
    amax = np.abs(w).max(1)
    if fmt == "e4m3":
        byte = np.frexp(amax)[1] - 1 + 127 - 7
    else:
        mant, ex = np.frexp(amax / 6.0)
        byte = np.where(mant > 0.5, ex, ex - 1) + 127
    byte = np.clip(np.where(amax > 0, byte, 1), 1, 254)
    scaled = (w * np.exp2(127.0 - byte)[:, None, :]).reshape(k, n).astype(np.float32)
    by_word = np.ascontiguousarray(scaled.reshape(k // 512, 128, 4, n).transpose(0, 1, 3, 2))
    if fmt == "e4m3":
        words = by_word.astype(ml_dtypes.float8_e4m3fn).view(np.uint8)
    else:
        c = by_word.astype(ml_dtypes.float4_e2m1fn).view(np.uint8) & 0xF
        words = c[..., 0::2] | (c[..., 1::2] << 4)
    return np.ascontiguousarray(words), np.ascontiguousarray(byte.astype(np.uint8).reshape(k // 512, 16, n))


def unpack_weight(words, scales, fmt):
    g, p, n, _ = words.shape
    if fmt == "e4m3":
        vals = np.ascontiguousarray(words).view(ml_dtypes.float8_e4m3fn).astype(np.float64)
    else:
        nib = np.empty((g, p, n, 4), np.uint8)
        nib[..., 0::2] = words & 0xF
        nib[..., 1::2] = words >> 4
        vals = E2M1[nib]
    vals = vals * np.repeat(np.exp2(scales.astype(np.float64) - 127.0), 8, axis=1)[..., None]
    return vals.transpose(0, 1, 3, 2).reshape(g * 512, n)


B, A, E, P, R = 256, 8, 512, 512, 512


def setup_inputs():
    s = mx_kscale(R)
    attr_rep = bf(np.random.standard_normal((B, A, R)) * s)
    stack = np.random.standard_normal((A, R, P)) / np.sqrt(R) / s[:, None]
    words, scales = pack_weight(stack.reshape(-1, P), "e4m3")
    self_weighted = bf(1.0 + 0.3 * np.random.standard_normal((1, A, 1)))
    return {
        "attr_rep": attr_rep,
        "bwd_proj_words": words,
        "bwd_proj_scales": scales,
        "self_weighted": self_weighted,
    }


def reference(attr_rep, bwd_proj_words, bwd_proj_scales, self_weighted):
    proj = (mxq(f64(attr_rep).transpose(1, 0, 2), 2, "e4m3") @ unpack_weight(bwd_proj_words, bwd_proj_scales, "e4m3").reshape(A, R, P)).transpose(1, 0, 2)
    return np.sum(np.maximum(proj, 0.0) * f64(self_weighted), axis=1)

@@ -1,0 +1,160 @@
+from contextlib import ExitStack
+
+import concourse.mybir as mybir
+from concourse.masks import make_identity
+
+BF16 = mybir.dt.bfloat16
+F32 = mybir.dt.float32
+I32 = mybir.dt.int32
+U32 = mybir.dt.uint32
+U8 = mybir.dt.uint8
+FP8X4 = mybir.dt.float8_e4m3fn_x4
+ALU = mybir.AluOpType
+ACT = mybir.ActivationFunctionType
+
+P = 128
+PACK = 4
+NODES = 256
+HALVES = NODES // P
+TYPES = 8
+K = 512
+N = 512
+WORDS = K // 2
+
+FLOPS = 2 * NODES * TYPES * K * N
+
+
+def tile_attributegnn_pb_e_kernel(
+    tc, attr_rep, bwd_proj_words, bwd_proj_scales, self_weighted, out
+):
+    nc = tc.nc
+    with ExitStack() as ctx:
+        const = ctx.enter_context(tc.tile_pool(name="const", bufs=1))
+        x_pool = ctx.enter_context(tc.tile_pool(name="x", bufs=TYPES))
+        w_pool = ctx.enter_context(tc.tile_pool(name="w", bufs=TYPES))
+        q_pool = ctx.enter_context(tc.tile_pool(name="q", bufs=3))
+        r_pool = ctx.enter_context(tc.tile_pool(name="r", bufs=4))
+        t_psum = ctx.enter_context(tc.psum_pool(name="t_psum", bufs=2))
+        mx_psum = ctx.enter_context(tc.psum_pool(name="mx_psum", bufs=6))
+
+        ident = const.tile([P, P], F32)
+        make_identity(nc, ident[:])
+
+        w_planes = const.tile([P, TYPES, N], U8, align_bytes=64)
+        nc.vector.memset(w_planes[:].rearrange("p a n -> p (a n)").bitcast(I32), 0)
+
+        sw_bf16 = const.tile([P, TYPES], BF16)
+        nc.scalar.dma_start(
+            out=sw_bf16[:],
+            in_=self_weighted.rearrange("o a i -> (o a i)").partition_broadcast(P),
+        )
+        sw = const.tile([P, TYPES], F32)
+        nc.vector.tensor_copy(out=sw[:], in_=sw_bf16[:])
+
+        x_view = attr_rep.rearrange("(h p) a k -> p h a k", p=P)
+        x_tiles = []
+        w_tiles = []
+
+        def load_x(a):
+            x_a = x_pool.tile([P, HALVES, K], BF16)
+            nc.sync.dma_start(out=x_a[:], in_=x_view[:, :, a, :])
+            x_tiles.append(x_a)
+
+        def load_w(a):
+            w_a = w_pool.tile([P, N * PACK], U8, align_bytes=64)
+            nc.sync.dma_start(
+                out=w_a[:].bitcast(I32),
+                in_=bwd_proj_words[a].rearrange("p n t -> p (n t)").bitcast(I32),
+            )
+            w_tiles.append(w_a)
+
+        load_x(0)
+        load_x(1)
+        for quad in range(4):
+            nc.sync.dma_start(
+                out=w_planes[32 * quad : 32 * quad + 4, :, :].bitcast(I32),
+                in_=bwd_proj_scales[:, 4 * quad : 4 * quad + 4, :]
+                .rearrange("a r n -> r a n")
+                .bitcast(I32),
+            )
+        load_w(0)
+        load_w(1)
+        for a in range(2, TYPES):
+            load_x(a)
+            load_w(a)
+
+        grouped_tiles = {}
+        code_tiles = {}
+        acc = []
+        for h in range(HALVES):
+            acc_h = const.tile([P, N], F32, name="acc%d" % h)
+            acc.append(acc_h)
+
+        def transpose_x(a):
+            x_words = x_tiles[a][:].bitcast(F32)
+            xt = t_psum.tile([P, HALVES, 2, P], F32)
+            for h in range(HALVES):
+                for u in range(2):
+                    nc.tensor.transpose(xt[:, h, u, :], x_words[:, h, u:WORDS:2], ident[:])
+            grouped = q_pool.tile([P, HALVES * P * PACK], BF16, align_bytes=64)
+            nc.scalar.copy(
+                out=grouped[:].bitcast(F32).rearrange("p (h b u) -> p h b u", h=HALVES, u=2),
+                in_=xt[:].rearrange("p h u b -> p h b u"),
+            )
+            grouped_tiles[a] = grouped
+
+        def quantise_x(a):
+            codes = q_pool.tile([P, HALVES * P], U32, align_bytes=64)
+            planes = q_pool.tile([P, HALVES * P], U8, align_bytes=64)
+            nc.vector.quantize_mx(
+                out=codes[:].bitcast(FP8X4), scales=planes[:], in_=grouped_tiles[a][:]
+            )
+            code_tiles[a] = (codes, planes)
+
+        def project_and_add(a):
+            codes, planes = code_tiles[a]
+            for h in range(HALVES):
+                cols = slice(h * P, (h + 1) * P)
+                proj = mx_psum.tile([P, N], F32)
+                nc.tensor.matmul_mx(
+                    out=proj[:],
+                    lhsT=codes[:, cols].bitcast(FP8X4),
+                    lhsT_scale=planes[:, cols],
+                    rhs=w_tiles[a][:].bitcast(FP8X4),
+                    rhs_scale=w_planes[:, a, :],
+                    start=True,
+                    stop=True,
+                )
+                if a == 0:
+                    nc.vector.tensor_scalar(
+                        out=acc[h][:],
+                        in0=proj[:],
+                        scalar1=0.0,
+                        scalar2=sw[:, 0:1],
+                        op0=ALU.max,
+                        op1=ALU.mult,
+                    )
+                else:
+                    relu = r_pool.tile([P, N], F32)
+                    nc.scalar.activation(out=relu[:], in_=proj[:], func=ACT.Relu)
+                    nc.vector.scalar_tensor_tensor(
+                        out=acc[h][:],
+                        in0=relu[:],
+                        scalar=sw[:, a : a + 1],
+                        in1=acc[h][:],
+                        op0=ALU.mult,
+                        op1=ALU.add,
+                    )
+
+        transpose_x(0)
+        transpose_x(1)
+        quantise_x(0)
+        for a in range(TYPES):
+            if a + 2 < TYPES:
+                transpose_x(a + 2)
+            if a + 1 < TYPES:
+                quantise_x(a + 1)
+            project_and_add(a)
+
+        for h in range(HALVES):
+            nc.sync.dma_start(out=out[h * P : (h + 1) * P, :], in_=acc[h][:])

@@ -19,6 +19,7 @@ HALVES = NODES // P
 TYPES = 8
 K = 512
 N = 512
+SHARE = 4
 WORDS = K // 2
 
 FLOPS = 2 * NODES * TYPES * K * N
@@ -40,8 +41,8 @@ def tile_attributegnn_pb_e_kernel(
         ident = const.tile([P, P], F32)
         make_identity(nc, ident[:])
 
-        w_planes = const.tile([P, TYPES, N], U8, align_bytes=64)
-        nc.vector.memset(w_planes[:].rearrange("p a n -> p (a n)").bitcast(I32), 0)
+        w_planes = const.tile([P, TYPES // SHARE, N], U8, align_bytes=64)
+        nc.vector.memset(w_planes[:].rearrange("p j n -> p (j n)").bitcast(I32), 0)
 
         sw_bf16 = const.tile([P, TYPES], BF16)
         nc.scalar.dma_start(
@@ -68,18 +69,23 @@ def tile_attributegnn_pb_e_kernel(
             )
             w_tiles.append(w_a)
 
+        def load_planes(j):
+            for quad in range(4):
+                nc.sync.dma_start(
+                    out=w_planes[32 * quad : 32 * quad + 4 * SHARE, j, :].bitcast(I32),
+                    in_=bwd_proj_scales[
+                        SHARE * j : SHARE * (j + 1), 4 * quad : 4 * quad + 4, :
+                    ].bitcast(I32),
+                )
+
         load_x(0)
         load_x(1)
-        for quad in range(4):
-            nc.sync.dma_start(
-                out=w_planes[32 * quad : 32 * quad + 4, :, :].bitcast(I32),
-                in_=bwd_proj_scales[:, 4 * quad : 4 * quad + 4, :]
-                .rearrange("a r n -> r a n")
-                .bitcast(I32),
-            )
+        load_planes(0)
         load_w(0)
         load_w(1)
         for a in range(2, TYPES):
+            if a % SHARE == 0:
+                load_planes(a // SHARE)
             load_x(a)
             load_w(a)
 
@@ -121,7 +127,7 @@ def tile_attributegnn_pb_e_kernel(
                     lhsT=codes[:, cols].bitcast(FP8X4),
                     lhsT_scale=planes[:, cols],
                     rhs=w_tiles[a][:].bitcast(FP8X4),
-                    rhs_scale=w_planes[:, a, :],
+                    rhs_scale=w_planes[4 * (a % SHARE) : P, a // SHARE, :],
                     start=True,
                     stop=True,
                 )

@@ -44,13 +44,15 @@ def tile_attributegnn_pb_e_kernel(
         w_planes = const.tile([P, TYPES // SHARE, N], U8, align_bytes=64)
         nc.vector.memset(w_planes[:].rearrange("p j n -> p (j n)").bitcast(I32), 0)
 
-        sw_bf16 = const.tile([P, TYPES], BF16)
-        nc.scalar.dma_start(
-            out=sw_bf16[:],
-            in_=self_weighted.rearrange("o a i -> (o a i)").partition_broadcast(P),
-        )
+        sw_rows = const.tile([P, TYPES], BF16)
+        nc.vector.memset(sw_rows[:], 0.0)
+        nc.scalar.dma_start(out=sw_rows[0:1, :], in_=self_weighted.rearrange("o a i -> o (a i)"))
+        ones = const.tile([P, P], BF16)
+        nc.vector.memset(ones[:], 1.0)
+        sw_psum = t_psum.tile([P, TYPES], F32, tag="xt")
+        nc.tensor.matmul(out=sw_psum[:], lhsT=ones[:], rhs=sw_rows[:], start=True, stop=True)
         sw = const.tile([P, TYPES], F32)
-        nc.vector.tensor_copy(out=sw[:], in_=sw_bf16[:])
+        nc.vector.tensor_copy(out=sw[:], in_=sw_psum[:])
 
         x_view = attr_rep.rearrange("(h p) a k -> p h a k", p=P)
         x_tiles = []

@@ -21,6 +21,8 @@ K = 512
 N = 512
 SHARE = 4
 WORDS = K // 2
+AHEAD = 2
+LOAD_AHEAD = AHEAD + 1
 
 FLOPS = 2 * NODES * TYPES * K * N
 
@@ -33,26 +35,24 @@ def tile_attributegnn_pb_e_kernel(
         const = ctx.enter_context(tc.tile_pool(name="const", bufs=1))
         x_pool = ctx.enter_context(tc.tile_pool(name="x", bufs=TYPES))
         w_pool = ctx.enter_context(tc.tile_pool(name="w", bufs=TYPES))
-        q_pool = ctx.enter_context(tc.tile_pool(name="q", bufs=3))
+        q_pool = ctx.enter_context(tc.tile_pool(name="q", bufs=AHEAD + 2))
         r_pool = ctx.enter_context(tc.tile_pool(name="r", bufs=4))
         t_psum = ctx.enter_context(tc.psum_pool(name="t_psum", bufs=2))
         mx_psum = ctx.enter_context(tc.psum_pool(name="mx_psum", bufs=6))
+        ctx.enter_context(tc.manual_schedule())
 
         ident = const.tile([P, P], F32)
         make_identity(nc, ident[:])
 
-        w_planes = const.tile([P, TYPES // SHARE, N], U8, align_bytes=64)
-        nc.vector.memset(w_planes[:].rearrange("p j n -> p (j n)").bitcast(I32), 0)
-
         sw_rows = const.tile([P, TYPES], BF16)
         nc.vector.memset(sw_rows[:], 0.0)
         nc.scalar.dma_start(out=sw_rows[0:1, :], in_=self_weighted.rearrange("o a i -> o (a i)"))
+
+        w_planes = const.tile([P, TYPES // SHARE, N], U8, align_bytes=64)
+        nc.vector.memset(w_planes[:].rearrange("p j n -> p (j n)").bitcast(I32), 0)
+
         ones = const.tile([P, P], BF16)
-        nc.vector.memset(ones[:], 1.0)
-        sw_psum = t_psum.tile([P, TYPES], F32, tag="xt")
-        nc.tensor.matmul(out=sw_psum[:], lhsT=ones[:], rhs=sw_rows[:], start=True, stop=True)
-        sw = const.tile([P, TYPES], F32)
-        nc.vector.tensor_copy(out=sw[:], in_=sw_psum[:])
+        nc.scalar.activation(out=ones[:], in_=ident[:], func=ACT.Copy, scale=0.0, bias=1.0)
 
         x_view = attr_rep.rearrange("(h p) a k -> p h a k", p=P)
         x_tiles = []
@@ -80,16 +80,14 @@ def tile_attributegnn_pb_e_kernel(
                     ].bitcast(I32),
                 )
 
-        load_x(0)
-        load_x(1)
-        load_planes(0)
-        load_w(0)
-        load_w(1)
-        for a in range(2, TYPES):
+        for a in range(LOAD_AHEAD):
+            load_x(a)
+        for a in range(TYPES):
             if a % SHARE == 0:
                 load_planes(a // SHARE)
-            load_x(a)
             load_w(a)
+            if a + LOAD_AHEAD < TYPES:
+                load_x(a + LOAD_AHEAD)
 
         grouped_tiles = {}
         code_tiles = {}
@@ -154,14 +152,20 @@ def tile_attributegnn_pb_e_kernel(
                         op1=ALU.add,
                     )
 
-        transpose_x(0)
-        transpose_x(1)
-        quantise_x(0)
+        for a in range(AHEAD):
+            transpose_x(a)
+
+        sw_psum = mx_psum.tile([P, TYPES], F32, tag="proj")
+        nc.tensor.matmul(out=sw_psum[:], lhsT=ones[:], rhs=sw_rows[:], start=True, stop=True)
+
+        for a in range(AHEAD):
+            quantise_x(a)
+        sw = const.tile([P, TYPES], F32)
+        nc.vector.tensor_copy(out=sw[:], in_=sw_psum[:])
         for a in range(TYPES):
-            if a + 2 < TYPES:
-                transpose_x(a + 2)
-            if a + 1 < TYPES:
-                quantise_x(a + 1)
+            if a + AHEAD < TYPES:
+                transpose_x(a + AHEAD)
+                quantise_x(a + AHEAD)
             project_and_add(a)
 
         for h in range(HALVES):

@@ -35,8 +35,8 @@ def tile_attributegnn_pb_e_kernel(
         const = ctx.enter_context(tc.tile_pool(name="const", bufs=1))
         x_pool = ctx.enter_context(tc.tile_pool(name="x", bufs=TYPES))
         w_pool = ctx.enter_context(tc.tile_pool(name="w", bufs=TYPES))
-        q_pool = ctx.enter_context(tc.tile_pool(name="q", bufs=AHEAD + 2))
-        r_pool = ctx.enter_context(tc.tile_pool(name="r", bufs=4))
+        q_pool = ctx.enter_context(tc.tile_pool(name="q", bufs=TYPES))
+        r_pool = ctx.enter_context(tc.tile_pool(name="r", bufs=TYPES * HALVES))
         t_psum = ctx.enter_context(tc.psum_pool(name="t_psum", bufs=2))
         mx_psum = ctx.enter_context(tc.psum_pool(name="mx_psum", bufs=6))
         ctx.enter_context(tc.manual_schedule())

@@ -23,6 +23,7 @@ SHARE = 4
 WORDS = K // 2
 AHEAD = 2
 LOAD_AHEAD = AHEAD + 1
+VECTOR_EVERY = 4
 
 FLOPS = 2 * NODES * TYPES * K * N
 
@@ -103,7 +104,8 @@ def tile_attributegnn_pb_e_kernel(
                 for u in range(2):
                     nc.tensor.transpose(xt[:, h, u, :], x_words[:, h, u:WORDS:2], ident[:])
             grouped = q_pool.tile([P, HALVES * P * PACK], BF16, align_bytes=64)
-            nc.scalar.copy(
+            copy = nc.vector.tensor_copy if a % VECTOR_EVERY == 0 else nc.scalar.copy
+            copy(
                 out=grouped[:].bitcast(F32).rearrange("p (h b u) -> p h b u", h=HALVES, u=2),
                 in_=xt[:].rearrange("p h u b -> p h b u"),
             )

@@ -24,6 +24,7 @@ WORDS = K // 2
 AHEAD = 2
 LOAD_AHEAD = AHEAD + 1
 VECTOR_EVERY = 4
+WARM_FRONT = 4
 
 FLOPS = 2 * NODES * TYPES * K * N
 
@@ -41,6 +42,18 @@ def tile_attributegnn_pb_e_kernel(
         t_psum = ctx.enter_context(tc.psum_pool(name="t_psum", bufs=2))
         mx_psum = ctx.enter_context(tc.psum_pool(name="mx_psum", bufs=6))
         ctx.enter_context(tc.manual_schedule())
+
+        warm = const.tile([P, N], BF16)
+        nc.vector.memset(warm[:], 0.0)
+        warm_psum = mx_psum.tile([P, N], F32, tag="proj")
+
+        def dummy():
+            nc.tensor.matmul(
+                out=warm_psum[:], lhsT=warm[:, 0:P], rhs=warm[:], start=True, stop=True
+            )
+
+        for i in range(WARM_FRONT):
+            dummy()
 
         ident = const.tile([P, P], F32)
         make_identity(nc, ident[:])
@@ -156,6 +169,7 @@ def tile_attributegnn_pb_e_kernel(
 
         for a in range(AHEAD):
             transpose_x(a)
+            dummy()
 
         sw_psum = mx_psum.tile([P, TYPES], F32, tag="proj")
         nc.tensor.matmul(out=sw_psum[:], lhsT=ones[:], rhs=sw_rows[:], start=True, stop=True)

@@ -21,10 +21,8 @@ K = 512
 N = 512
 SHARE = 4
 WORDS = K // 2
-AHEAD = 2
-LOAD_AHEAD = AHEAD + 1
-VECTOR_EVERY = 4
-WARM_FRONT = 4
+PROGRAM = "D0 D0 D0 D0 T0 D0 c0 T1 D0 C1 o0 Q0 Q1 s0 T2 C2 Q2 M0 R0 M1 R1 T3 C3 Q3 T4 c4 Q4 M2 R2 T5 C5 Q5 M3 R3 T6 C6 Q6 M4 R4 T7 C7 Q7 M5 R5 M6 R6 M7 R7"
+LOAD_ORDER = "x0 x1 x2 p0 w0 w1 x3 x4 w2 x5 w3 x6 p1 w4 x7 w5 w6 w7"
 
 FLOPS = 2 * NODES * TYPES * K * N
 
@@ -51,9 +49,6 @@ def tile_attributegnn_pb_e_kernel(
             nc.tensor.matmul(
                 out=warm_psum[:], lhsT=warm[:, 0:P], rhs=warm[:], start=True, stop=True
             )
-
-        for i in range(WARM_FRONT):
-            dummy()
 
         ident = const.tile([P, P], F32)
         make_identity(nc, ident[:])
@@ -94,15 +89,16 @@ def tile_attributegnn_pb_e_kernel(
                     ].bitcast(I32),
                 )
 
-        for a in range(LOAD_AHEAD):
-            load_x(a)
-        for a in range(TYPES):
-            if a % SHARE == 0:
-                load_planes(a // SHARE)
-            load_w(a)
-            if a + LOAD_AHEAD < TYPES:
-                load_x(a + LOAD_AHEAD)
+        for name in LOAD_ORDER.split():
+            if name[0] == "x":
+                load_x(int(name[1]))
+            elif name[0] == "w":
+                load_w(int(name[1]))
+            else:
+                load_planes(int(name[1]))
 
+        xt_tiles = {}
+        proj_tiles = {}
         grouped_tiles = {}
         code_tiles = {}
         acc = []
@@ -116,8 +112,11 @@ def tile_attributegnn_pb_e_kernel(
             for h in range(HALVES):
                 for u in range(2):
                     nc.tensor.transpose(xt[:, h, u, :], x_words[:, h, u:WORDS:2], ident[:])
+            xt_tiles[a] = xt
+
+        def group_x(a, copy):
+            xt = xt_tiles[a]
             grouped = q_pool.tile([P, HALVES * P * PACK], BF16, align_bytes=64)
-            copy = nc.vector.tensor_copy if a % VECTOR_EVERY == 0 else nc.scalar.copy
             copy(
                 out=grouped[:].bitcast(F32).rearrange("p (h b u) -> p h b u", h=HALVES, u=2),
                 in_=xt[:].rearrange("p h u b -> p h b u"),
@@ -132,11 +131,12 @@ def tile_attributegnn_pb_e_kernel(
             )
             code_tiles[a] = (codes, planes)
 
-        def project_and_add(a):
+        def project(a):
             codes, planes = code_tiles[a]
             for h in range(HALVES):
                 cols = slice(h * P, (h + 1) * P)
                 proj = mx_psum.tile([P, N], F32)
+                proj_tiles[(a, h)] = proj
                 nc.tensor.matmul_mx(
                     out=proj[:],
                     lhsT=codes[:, cols].bitcast(FP8X4),
@@ -146,6 +146,10 @@ def tile_attributegnn_pb_e_kernel(
                     start=True,
                     stop=True,
                 )
+
+        def relu_and_add(a):
+            for h in range(HALVES):
+                proj = proj_tiles[(a, h)]
                 if a == 0:
                     nc.vector.tensor_scalar(
                         out=acc[h][:],
@@ -167,22 +171,28 @@ def tile_attributegnn_pb_e_kernel(
                         op1=ALU.add,
                     )
 
-        for a in range(AHEAD):
-            transpose_x(a)
-            dummy()
-
         sw_psum = mx_psum.tile([P, TYPES], F32, tag="proj")
-        nc.tensor.matmul(out=sw_psum[:], lhsT=ones[:], rhs=sw_rows[:], start=True, stop=True)
-
-        for a in range(AHEAD):
-            quantise_x(a)
         sw = const.tile([P, TYPES], F32)
-        nc.vector.tensor_copy(out=sw[:], in_=sw_psum[:])
-        for a in range(TYPES):
-            if a + AHEAD < TYPES:
-                transpose_x(a + AHEAD)
-                quantise_x(a + AHEAD)
-            project_and_add(a)
+
+        def spread_weights(a):
+            nc.tensor.matmul(out=sw_psum[:], lhsT=ones[:], rhs=sw_rows[:], start=True, stop=True)
+
+        def keep_weights(a):
+            nc.vector.tensor_copy(out=sw[:], in_=sw_psum[:])
+
+        steps = {
+            "D": lambda a: dummy(),
+            "T": transpose_x,
+            "C": lambda a: group_x(a, nc.scalar.copy),
+            "c": lambda a: group_x(a, nc.vector.tensor_copy),
+            "Q": quantise_x,
+            "M": project,
+            "R": relu_and_add,
+            "o": spread_weights,
+            "s": keep_weights,
+        }
+        for step in PROGRAM.split():
+            steps[step[0]](int(step[1]))
 
         for h in range(HALVES):
             nc.sync.dma_start(out=out[h * P : (h + 1) * P, :], in_=acc[h][:])

@@ -57,8 +57,11 @@ def tile_attributegnn_pb_e_kernel(
         nc.vector.memset(sw_rows[:], 0.0)
         nc.scalar.dma_start(out=sw_rows[0:1, :], in_=self_weighted.rearrange("o a i -> o (a i)"))
 
-        w_planes = const.tile([P, TYPES // SHARE, N], U8, align_bytes=64)
-        nc.vector.memset(w_planes[:].rearrange("p j n -> p (j n)").bitcast(I32), 0)
+        w_planes = [
+            const.tile([P, N], U8, align_bytes=64, name="planes%d" % j)
+            for j in range(TYPES // SHARE)
+        ]
+        nc.vector.memset(w_planes[1][:].bitcast(I32), 0)
 
         ones = const.tile([P, P], BF16)
         nc.scalar.activation(out=ones[:], in_=ident[:], func=ACT.Copy, scale=0.0, bias=1.0)
@@ -83,9 +86,9 @@ def tile_attributegnn_pb_e_kernel(
         def load_planes(j):
             for quad in range(4):
                 nc.sync.dma_start(
-                    out=w_planes[32 * quad : 32 * quad + 4 * SHARE, j, :].bitcast(I32),
+                    out=w_planes[j][32 * quad : 32 * quad + 4 * (TYPES - SHARE * j), :].bitcast(I32),
                     in_=bwd_proj_scales[
-                        SHARE * j : SHARE * (j + 1), 4 * quad : 4 * quad + 4, :
+                        SHARE * j : TYPES, 4 * quad : 4 * quad + 4, :
                     ].bitcast(I32),
                 )
 
@@ -142,7 +145,7 @@ def tile_attributegnn_pb_e_kernel(
                     lhsT=codes[:, cols].bitcast(FP8X4),
                     lhsT_scale=planes[:, cols],
                     rhs=w_tiles[a][:].bitcast(FP8X4),
-                    rhs_scale=w_planes[4 * (a % SHARE) : P, a // SHARE, :],
+                    rhs_scale=w_planes[a // SHARE][4 * (a % SHARE) : P, :],
                     start=True,
                     stop=True,
                 )

@@ -13,6 +13,7 @@ ALU = mybir.AluOpType
 ACT = mybir.ActivationFunctionType
 
 P = 128
+PIECES = 2
 PACK = 4
 NODES = 256
 HALVES = NODES // P
@@ -21,7 +22,7 @@ K = 512
 N = 512
 SHARE = 4
 WORDS = K // 2
-PROGRAM = "D0 D0 D0 D0 T0 D0 c0 T1 D0 C1 o0 Q0 Q1 s0 T2 C2 Q2 M0 R0 M1 R1 T3 C3 Q3 T4 c4 Q4 M2 R2 T5 C5 Q5 M3 R3 T6 C6 Q6 M4 R4 T7 C7 Q7 M5 R5 M6 R6 M7 R7"
+PROGRAM = "D0 D0 D0 D0 T0 D0 c0 T1 D0 C1 o0 Q0 Q1 s0 T2 C2 M0 R0a Q2 R0b M1 r1 a1 T3 C3 Q3 T4 c4 Q4 M2 r2 a2 T5 C5 Q5 M3 r3 a3 T6 C6 Q6 M4 r4 a4 T7 C7 Q7 M5 r5 a5 M6 r6 a6 M7 r7 e7"
 LOAD_ORDER = "x0 x1 x2 p0 w0 w1 x3 x4 w2 x5 w3 x6 p1 w4 x7 w5 w6 w7"
 
 FLOPS = 2 * NODES * TYPES * K * N
@@ -104,12 +105,13 @@ def tile_attributegnn_pb_e_kernel(
         proj_tiles = {}
         grouped_tiles = {}
         code_tiles = {}
+        relu_tiles = {}
         acc = []
         for h in range(HALVES):
             acc_h = const.tile([P, N], F32, name="acc%d" % h)
             acc.append(acc_h)
 
-        def transpose_x(a):
+        def transpose_x(a, halves):
             x_words = x_tiles[a][:].bitcast(F32)
             xt = t_psum.tile([P, HALVES, 2, P], F32)
             for h in range(HALVES):
@@ -126,7 +128,7 @@ def tile_attributegnn_pb_e_kernel(
             )
             grouped_tiles[a] = grouped
 
-        def quantise_x(a):
+        def quantise_x(a, halves):
             codes = q_pool.tile([P, HALVES * P], U32, align_bytes=64)
             planes = q_pool.tile([P, HALVES * P], U8, align_bytes=64)
             nc.vector.quantize_mx(
@@ -134,9 +136,9 @@ def tile_attributegnn_pb_e_kernel(
             )
             code_tiles[a] = (codes, planes)
 
-        def project(a):
+        def project(a, halves):
             codes, planes = code_tiles[a]
-            for h in range(HALVES):
+            for h in halves:
                 cols = slice(h * P, (h + 1) * P)
                 proj = mx_psum.tile([P, N], F32)
                 proj_tiles[(a, h)] = proj
@@ -150,52 +152,71 @@ def tile_attributegnn_pb_e_kernel(
                     stop=True,
                 )
 
-        def relu_and_add(a):
-            for h in range(HALVES):
-                proj = proj_tiles[(a, h)]
-                if a == 0:
-                    nc.vector.tensor_scalar(
-                        out=acc[h][:],
-                        in0=proj[:],
-                        scalar1=0.0,
-                        scalar2=sw[:, 0:1],
-                        op0=ALU.max,
-                        op1=ALU.mult,
-                    )
-                else:
-                    relu = r_pool.tile([P, N], F32)
-                    nc.scalar.activation(out=relu[:], in_=proj[:], func=ACT.Relu)
+        def relu_and_weigh(a, halves):
+            for h in halves:
+                nc.vector.tensor_scalar(
+                    out=acc[h][:],
+                    in0=proj_tiles[(a, h)][:],
+                    scalar1=0.0,
+                    scalar2=sw[:, a : a + 1],
+                    op0=ALU.max,
+                    op1=ALU.mult,
+                )
+
+        def take_relu(a, halves):
+            for h in halves:
+                relu = r_pool.tile([P, N], F32)
+                nc.scalar.activation(out=relu[:], in_=proj_tiles[(a, h)][:], func=ACT.Relu)
+                relu_tiles[(a, h)] = relu
+
+        def weigh_and_add(a, halves):
+            for h in halves:
+                nc.vector.scalar_tensor_tensor(
+                    out=acc[h][:],
+                    in0=relu_tiles[(a, h)][:],
+                    scalar=sw[:, a : a + 1],
+                    in1=acc[h][:],
+                    op0=ALU.mult,
+                    op1=ALU.add,
+                )
+
+        def add_and_store(a, halves):
+            for h in halves:
+                pieces = PIECES if h == HALVES - 1 else 1
+                for i in range(pieces):
+                    cols = slice(i * N // pieces, (i + 1) * N // pieces)
                     nc.vector.scalar_tensor_tensor(
-                        out=acc[h][:],
-                        in0=relu[:],
+                        out=acc[h][:, cols],
+                        in0=relu_tiles[(a, h)][:, cols],
                         scalar=sw[:, a : a + 1],
-                        in1=acc[h][:],
+                        in1=acc[h][:, cols],
                         op0=ALU.mult,
                         op1=ALU.add,
                     )
+                    nc.sync.dma_start(out=out[h * P : (h + 1) * P, cols], in_=acc[h][:, cols])
 
         sw_psum = mx_psum.tile([P, TYPES], F32, tag="proj")
         sw = const.tile([P, TYPES], F32)
 
-        def spread_weights(a):
+        def spread_weights(a, halves):
             nc.tensor.matmul(out=sw_psum[:], lhsT=ones[:], rhs=sw_rows[:], start=True, stop=True)
 
-        def keep_weights(a):
+        def keep_weights(a, halves):
             nc.vector.tensor_copy(out=sw[:], in_=sw_psum[:])
 
         steps = {
-            "D": lambda a: dummy(),
+            "D": lambda a, halves: dummy(),
             "T": transpose_x,
-            "C": lambda a: group_x(a, nc.scalar.copy),
-            "c": lambda a: group_x(a, nc.vector.tensor_copy),
+            "C": lambda a, halves: group_x(a, nc.scalar.copy),
+            "c": lambda a, halves: group_x(a, nc.vector.tensor_copy),
             "Q": quantise_x,
             "M": project,
-            "R": relu_and_add,
+            "R": relu_and_weigh,
+            "r": take_relu,
+            "a": weigh_and_add,
+            "e": add_and_store,
             "o": spread_weights,
             "s": keep_weights,
         }
         for step in PROGRAM.split():
-            steps[step[0]](int(step[1]))
-
-        for h in range(HALVES):
-            nc.sync.dma_start(out=out[h * P : (h + 1) * P, :], in_=acc[h][:])
+            steps[step[0]](int(step[1]), {"": (0, 1), "a": (0,), "b": (1,)}[step[2:]])

@@ -22,7 +22,7 @@ K = 512
 N = 512
 SHARE = 4
 WORDS = K // 2
-PROGRAM = "D0 D0 D0 D0 T0 D0 c0 T1 D0 C1 o0 Q0 Q1 s0 T2 C2 M0 R0a Q2 R0b M1 r1 a1 T3 C3 Q3 T4 c4 Q4 M2 r2 a2 T5 C5 Q5 M3 r3 a3 T6 C6 Q6 M4 r4 a4 T7 C7 Q7 M5 r5 a5 M6 r6 a6 M7 r7 e7"
+PROGRAM = "D0 D0 D0 D0 F0 T0 F0 c0 T1 F0 C1 o0 Q0 Q1 s0 T2 F0 C2 M0 R0a Q2 R0b M1 r1 a1 T3 C3 Q3 T4 c4 Q4 M2 r2 a2 T5 C5 Q5 M3 r3 a3 T6 C6 Q6 M4 r4 a4 T7 C7 Q7 M5 r5 a5 M6 r6 a6 M7 r7 e7"
 LOAD_ORDER = "x0 x1 x2 p0 w0 w1 x3 x4 w2 x5 w3 x6 p1 w4 x7 w5 w6 w7"
 
 FLOPS = 2 * NODES * TYPES * K * N
@@ -53,6 +53,11 @@ def tile_attributegnn_pb_e_kernel(
 
         ident = const.tile([P, P], F32)
         make_identity(nc, ident[:])
+
+        def dummy_f32():
+            nc.tensor.matmul(
+                out=warm_psum[:, 0:P], lhsT=ident[:], rhs=ident[:], start=True, stop=True
+            )
 
         sw_rows = const.tile([P, TYPES], BF16)
         nc.vector.memset(sw_rows[:], 0.0)
@@ -206,6 +211,7 @@ def tile_attributegnn_pb_e_kernel(
 
         steps = {
             "D": lambda a, halves: dummy(),
+            "F": lambda a, halves: dummy_f32(),
             "T": transpose_x,
             "C": lambda a, halves: group_x(a, nc.scalar.copy),
             "c": lambda a, halves: group_x(a, nc.vector.tensor_copy),

from contextlib import ExitStack

import concourse.mybir as mybir
from concourse.masks import make_identity

BF16 = mybir.dt.bfloat16
F32 = mybir.dt.float32
I32 = mybir.dt.int32
U32 = mybir.dt.uint32
U8 = mybir.dt.uint8
FP8X4 = mybir.dt.float8_e4m3fn_x4
ALU = mybir.AluOpType
ACT = mybir.ActivationFunctionType

P = 128
PIECES = 2
PACK = 4
NODES = 256
HALVES = NODES // P
TYPES = 8
K = 512
N = 512
SHARE = 4
WORDS = K // 2
PROGRAM = "D0 D0 D0 D0 F0 T0 F0 c0 T1 F0 C1 o0 Q0 Q1 s0 T2 F0 C2 M0 R0a Q2 R0b M1 r1 a1 T3 C3 Q3 T4 c4 Q4 M2 r2 a2 T5 C5 Q5 M3 r3 a3 T6 C6 Q6 M4 r4 a4 T7 C7 Q7 M5 r5 a5 M6 r6 a6 M7 r7 e7"
LOAD_ORDER = "x0 x1 x2 p0 w0 w1 x3 x4 w2 x5 w3 x6 p1 w4 x7 w5 w6 w7"

FLOPS = 2 * NODES * TYPES * K * N


def tile_attributegnn_pb_e_kernel(
    tc, attr_rep, bwd_proj_words, bwd_proj_scales, self_weighted, out
):
    nc = tc.nc
    with ExitStack() as ctx:
        const = ctx.enter_context(tc.tile_pool(name="const", bufs=1))
        x_pool = ctx.enter_context(tc.tile_pool(name="x", bufs=TYPES))
        w_pool = ctx.enter_context(tc.tile_pool(name="w", bufs=TYPES))
        q_pool = ctx.enter_context(tc.tile_pool(name="q", bufs=TYPES))
        r_pool = ctx.enter_context(tc.tile_pool(name="r", bufs=TYPES * HALVES))
        t_psum = ctx.enter_context(tc.psum_pool(name="t_psum", bufs=2))
        mx_psum = ctx.enter_context(tc.psum_pool(name="mx_psum", bufs=6))
        ctx.enter_context(tc.manual_schedule())

        warm = const.tile([P, N], BF16)
        nc.vector.memset(warm[:], 0.0)
        warm_psum = mx_psum.tile([P, N], F32, tag="proj")

        def dummy():
            nc.tensor.matmul(
                out=warm_psum[:], lhsT=warm[:, 0:P], rhs=warm[:], start=True, stop=True
            )

        ident = const.tile([P, P], F32)
        make_identity(nc, ident[:])

        def dummy_f32():
            nc.tensor.matmul(
                out=warm_psum[:, 0:P], lhsT=ident[:], rhs=ident[:], start=True, stop=True
            )

        sw_rows = const.tile([P, TYPES], BF16)
        nc.vector.memset(sw_rows[:], 0.0)
        nc.scalar.dma_start(out=sw_rows[0:1, :], in_=self_weighted.rearrange("o a i -> o (a i)"))

        w_planes = [
            const.tile([P, N], U8, align_bytes=64, name="planes%d" % j)
            for j in range(TYPES // SHARE)
        ]
        nc.vector.memset(w_planes[1][:].bitcast(I32), 0)

        ones = const.tile([P, P], BF16)
        nc.scalar.activation(out=ones[:], in_=ident[:], func=ACT.Copy, scale=0.0, bias=1.0)

        x_view = attr_rep.rearrange("(h p) a k -> p h a k", p=P)
        x_tiles = []
        w_tiles = []

        def load_x(a):
            x_a = x_pool.tile([P, HALVES, K], BF16)
            nc.sync.dma_start(out=x_a[:], in_=x_view[:, :, a, :])
            x_tiles.append(x_a)

        def load_w(a):
            w_a = w_pool.tile([P, N * PACK], U8, align_bytes=64)
            nc.sync.dma_start(
                out=w_a[:].bitcast(I32),
                in_=bwd_proj_words[a].rearrange("p n t -> p (n t)").bitcast(I32),
            )
            w_tiles.append(w_a)

        def load_planes(j):
            for quad in range(4):
                nc.sync.dma_start(
                    out=w_planes[j][32 * quad : 32 * quad + 4 * (TYPES - SHARE * j), :].bitcast(I32),
                    in_=bwd_proj_scales[
                        SHARE * j : TYPES, 4 * quad : 4 * quad + 4, :
                    ].bitcast(I32),
                )

        for name in LOAD_ORDER.split():
            if name[0] == "x":
                load_x(int(name[1]))
            elif name[0] == "w":
                load_w(int(name[1]))
            else:
                load_planes(int(name[1]))

        xt_tiles = {}
        proj_tiles = {}
        grouped_tiles = {}
        code_tiles = {}
        relu_tiles = {}
        acc = []
        for h in range(HALVES):
            acc_h = const.tile([P, N], F32, name="acc%d" % h)
            acc.append(acc_h)

        def transpose_x(a, halves):
            x_words = x_tiles[a][:].bitcast(F32)
            xt = t_psum.tile([P, HALVES, 2, P], F32)
            for h in range(HALVES):
                for u in range(2):
                    nc.tensor.transpose(xt[:, h, u, :], x_words[:, h, u:WORDS:2], ident[:])
            xt_tiles[a] = xt

        def group_x(a, copy):
            xt = xt_tiles[a]
            grouped = q_pool.tile([P, HALVES * P * PACK], BF16, align_bytes=64)
            copy(
                out=grouped[:].bitcast(F32).rearrange("p (h b u) -> p h b u", h=HALVES, u=2),
                in_=xt[:].rearrange("p h u b -> p h b u"),
            )
            grouped_tiles[a] = grouped

        def quantise_x(a, halves):
            codes = q_pool.tile([P, HALVES * P], U32, align_bytes=64)
            planes = q_pool.tile([P, HALVES * P], U8, align_bytes=64)
            nc.vector.quantize_mx(
                out=codes[:].bitcast(FP8X4), scales=planes[:], in_=grouped_tiles[a][:]
            )
            code_tiles[a] = (codes, planes)

        def project(a, halves):
            codes, planes = code_tiles[a]
            for h in halves:
                cols = slice(h * P, (h + 1) * P)
                proj = mx_psum.tile([P, N], F32)
                proj_tiles[(a, h)] = proj
                nc.tensor.matmul_mx(
                    out=proj[:],
                    lhsT=codes[:, cols].bitcast(FP8X4),
                    lhsT_scale=planes[:, cols],
                    rhs=w_tiles[a][:].bitcast(FP8X4),
                    rhs_scale=w_planes[a // SHARE][4 * (a % SHARE) : P, :],
                    start=True,
                    stop=True,
                )

        def relu_and_weigh(a, halves):
            for h in halves:
                nc.vector.tensor_scalar(
                    out=acc[h][:],
                    in0=proj_tiles[(a, h)][:],
                    scalar1=0.0,
                    scalar2=sw[:, a : a + 1],
                    op0=ALU.max,
                    op1=ALU.mult,
                )

        def take_relu(a, halves):
            for h in halves:
                relu = r_pool.tile([P, N], F32)
                nc.scalar.activation(out=relu[:], in_=proj_tiles[(a, h)][:], func=ACT.Relu)
                relu_tiles[(a, h)] = relu

        def weigh_and_add(a, halves):
            for h in halves:
                nc.vector.scalar_tensor_tensor(
                    out=acc[h][:],
                    in0=relu_tiles[(a, h)][:],
                    scalar=sw[:, a : a + 1],
                    in1=acc[h][:],
                    op0=ALU.mult,
                    op1=ALU.add,
                )

        def add_and_store(a, halves):
            for h in halves:
                pieces = PIECES if h == HALVES - 1 else 1
                for i in range(pieces):
                    cols = slice(i * N // pieces, (i + 1) * N // pieces)
                    nc.vector.scalar_tensor_tensor(
                        out=acc[h][:, cols],
                        in0=relu_tiles[(a, h)][:, cols],
                        scalar=sw[:, a : a + 1],
                        in1=acc[h][:, cols],
                        op0=ALU.mult,
                        op1=ALU.add,
                    )
                    nc.sync.dma_start(out=out[h * P : (h + 1) * P, cols], in_=acc[h][:, cols])

        sw_psum = mx_psum.tile([P, TYPES], F32, tag="proj")
        sw = const.tile([P, TYPES], F32)

        def spread_weights(a, halves):
            nc.tensor.matmul(out=sw_psum[:], lhsT=ones[:], rhs=sw_rows[:], start=True, stop=True)

        def keep_weights(a, halves):
            nc.vector.tensor_copy(out=sw[:], in_=sw_psum[:])

        steps = {
            "D": lambda a, halves: dummy(),
            "F": lambda a, halves: dummy_f32(),
            "T": transpose_x,
            "C": lambda a, halves: group_x(a, nc.scalar.copy),
            "c": lambda a, halves: group_x(a, nc.vector.tensor_copy),
            "Q": quantise_x,
            "M": project,
            "R": relu_and_weigh,
            "r": take_relu,
            "a": weigh_and_add,
            "e": add_and_store,
            "o": spread_weights,
            "s": keep_weights,
        }
        for step in PROGRAM.split():
            steps[step[0]](int(step[1]), {"": (0, 1), "a": (0,), "b": (1,)}[step[2:]])
